import numpy as np
import ml_dtypes


def mxq(x, axis, fmt="e4m3"):
    dtype, down = {"e4m3": (ml_dtypes.float8_e4m3fn, 7), "e5m2": (ml_dtypes.float8_e5m2, 14)}[fmt]
    v = np.moveaxis(np.asarray(x, np.float32).astype(ml_dtypes.bfloat16).astype(np.float64), axis, -1)
    blocks = v.reshape(v.shape[:-1] + (-1, 32))
    amax = np.abs(blocks).max(-1, keepdims=True)
    byte = np.maximum(np.where(amax > 0, np.frexp(amax)[1] - 1 + 127, 0) - down, 1)
    scale = np.exp2(byte - 127.0)
    codes = (blocks / scale).astype(np.float32).astype(dtype).astype(np.float64)
    return np.moveaxis((codes * scale).reshape(v.shape), -1, axis)


WIDE = False


def mx_kscale(k):
    if not WIDE:
        return np.ones(k)
    levels = np.array([10, -10, 5, -5, 0])
    a = np.random.permutation(np.resize(levels, k // 512 * 4)).reshape(k // 512, 4)
    idx = np.arange(k)
    return np.exp2(a[idx // 512, idx % 128 // 32])


BF16 = ml_dtypes.bfloat16


def bf(x):
    return np.asarray(x, np.float32).astype(BF16)


def f64(x):
    return np.asarray(x).astype(np.float64)


B, N, D, H, DK, DV = 4, 4096, 512, 4, 64, 64


def xnorm(x, g):
    n = np.sqrt(np.sum(x * x, axis=-1, keepdims=True))
    return x * g / n


def setup_inputs():
    s = mx_kscale(D)
    return {
        "queries": bf(np.random.standard_normal((B, N, D)) * s),
        "Wq": bf(np.random.standard_normal((D, H * DK)) / np.sqrt(D) / s[:, None]),
        "bq": bf(np.random.standard_normal(H * DK) * 0.1),
        "gamma": bf(np.random.standard_normal((1, H, 1, 1)) * 2.0),
    }


def reference(queries, Wq, bq, gamma):
    q = ((mxq(f64(queries), 2, "e4m3") @ mxq(f64(Wq), 0, "e4m3")) + f64(bq)).reshape(B, N, H, DK)
    return xnorm(q.transpose(0, 2, 1, 3), f64(gamma))

@@ -1,0 +1,174 @@
+from contextlib import ExitStack
+
+import concourse.mybir as mybir
+from concourse.masks import make_identity
+
+F32 = mybir.dt.float32
+BF16 = mybir.dt.bfloat16
+U32 = mybir.dt.uint32
+U8 = mybir.dt.uint8
+FP8X4 = mybir.dt.float8_e4m3fn_x4
+ACT = mybir.ActivationFunctionType
+ALU = mybir.AluOpType
+
+P = 128
+BATCH, TOKENS, K = 4, 4096, 512
+HEADS, HEAD_DIM = 4, 64
+OUT_COLS = HEADS * HEAD_DIM
+PACK = 4
+WORDS = K // 2
+
+TILES = 8
+CHUNK_TOKENS = P * TILES
+CHUNKS = BATCH * TOKENS // CHUNK_TOKENS
+CHUNKS_PER_BATCH = TOKENS // CHUNK_TOKENS
+BANK_TILES = 2
+BANKS = TILES // BANK_TILES
+QUANT_TILES = 4
+
+FLOPS = 2 * BATCH * TOKENS * K * OUT_COLS
+
+
+def tile_ufoattention_pb_t_kernel(tc, queries, Wq, bq, gamma, out):
+    nc = tc.nc
+    with ExitStack() as ctx:
+        const = ctx.enter_context(tc.tile_pool(name="const", bufs=1))
+        x_pool = ctx.enter_context(tc.tile_pool(name="x", bufs=6))
+        mx_pool = ctx.enter_context(tc.tile_pool(name="mx", bufs=3))
+        q_pool = ctx.enter_context(tc.tile_pool(name="q", bufs=4))
+        small = ctx.enter_context(tc.tile_pool(name="small", bufs=3))
+        psum_t = ctx.enter_context(tc.psum_pool(name="psum_t", bufs=4))
+        psum_q = ctx.enter_context(tc.psum_pool(name="psum_q", bufs=4))
+
+        x_chunks = queries.flatten_outer_dims().rearrange(
+            "(c p j) k -> c p (j k)", p=P, j=TILES
+        )
+
+        one = const.tile([P, 1], F32)
+        nc.vector.memset(one[:], 1.0)
+        nc.scalar.activation(out=one[:], in_=one[:], func=ACT.Sqrt)
+
+        ident = const.tile([P, P], F32)
+        make_identity(nc, ident[:])
+
+        w_raw = const.tile([P, PACK, OUT_COLS], BF16)
+        nc.scalar.dma_start(
+            out=w_raw[:].rearrange("p (u e) c -> p u (e c)", u=2),
+            in_=Wq.rearrange("(u p e) c -> p u (e c)", u=2, e=2),
+        )
+        w_grouped = const.tile([P, OUT_COLS, PACK], BF16, align_bytes=64)
+        nc.vector.tensor_copy(out=w_grouped[:], in_=w_raw[:].rearrange("p t c -> p c t"))
+        w_codes = const.tile([P, OUT_COLS], U32, align_bytes=64)
+        w_scales = const.tile([P, OUT_COLS], U8, align_bytes=64)
+        nc.vector.quantize_mx(
+            out=w_codes[:].bitcast(FP8X4),
+            scales=w_scales[:],
+            in_=w_grouped[:].rearrange("p c t -> p (c t)"),
+        )
+
+        bias_bf = const.tile([P, OUT_COLS], BF16)
+        nc.scalar.dma_start(out=bias_bf[:], in_=bq.partition_broadcast(P))
+        bias_bank = const.tile([P, HEADS, BANK_TILES, HEAD_DIM], F32)
+        for i in range(BANK_TILES):
+            nc.vector.tensor_copy(
+                out=bias_bank[:, :, i, :],
+                in_=bias_bf[:].rearrange("p (h d) -> p h d", h=HEADS),
+            )
+
+        gamma_bf = const.tile([P, HEADS], BF16)
+        nc.scalar.dma_start(
+            out=gamma_bf[:],
+            in_=gamma.rearrange("a h b c -> (a h b c)").partition_broadcast(P),
+        )
+        gamma_chunk = const.tile([P, HEADS, TILES], F32)
+        nc.vector.tensor_copy(
+            out=gamma_chunk[:],
+            in_=gamma_bf[:].unsqueeze(2).to_broadcast([P, HEADS, TILES]),
+        )
+
+        squares = const.tile([P, HEAD_DIM], F32)
+
+        for c in range(CHUNKS):
+            x_sb = x_pool.tile([P, TILES * K], BF16)
+            nc.sync.dma_start(out=x_sb[:], in_=x_chunks[c])
+            x_words = x_sb[:].bitcast(F32)
+
+            grouped = mx_pool.tile([P, TILES * K], BF16, align_bytes=64)
+            grouped_words = grouped[:].bitcast(F32)
+            for bank in range(BANKS):
+                xt = psum_t.tile([P, BANK_TILES, 2, P], F32)
+                for i in range(BANK_TILES):
+                    j = bank * BANK_TILES + i
+                    for u in range(2):
+                        first = j * WORDS + u * P
+                        nc.tensor.transpose(xt[:, i, u, :], x_words[:, first : first + P], ident[:])
+                dst = grouped_words[
+                    :, bank * BANK_TILES * WORDS : (bank + 1) * BANK_TILES * WORDS
+                ].rearrange("p (i r u) -> p i r u", i=BANK_TILES, u=2)
+                src = xt[:].rearrange("p i u r -> p i r u")
+                if bank % 2 == 0:
+                    nc.scalar.copy(out=dst, in_=src)
+                else:
+                    nc.vector.tensor_copy(out=dst, in_=src)
+
+            codes = mx_pool.tile([P, TILES * P], U32, align_bytes=64)
+            scales = mx_pool.tile([P, TILES * P], U8, align_bytes=64)
+            for g in range(TILES // QUANT_TILES):
+                cols = slice(g * QUANT_TILES * P, (g + 1) * QUANT_TILES * P)
+                nc.vector.quantize_mx(
+                    out=codes[:, cols].bitcast(FP8X4),
+                    scales=scales[:, cols],
+                    in_=grouped[:, g * QUANT_TILES * K : (g + 1) * QUANT_TILES * K],
+                )
+
+            q_sb = q_pool.tile([P, HEADS, TILES, HEAD_DIM], F32)
+            for bank in range(BANKS):
+                acc = psum_q.tile([P, BANK_TILES, OUT_COLS], F32)
+                for i in range(BANK_TILES):
+                    j = bank * BANK_TILES + i
+                    nc.tensor.matmul_mx(
+                        out=acc[:, i, :],
+                        lhsT=codes[:, j * P : (j + 1) * P].bitcast(FP8X4),
+                        lhsT_scale=scales[:, j * P : (j + 1) * P],
+                        rhs=w_codes[:].bitcast(FP8X4),
+                        rhs_scale=w_scales[:],
+                        start=True,
+                        stop=True,
+                    )
+                nc.vector.tensor_tensor(
+                    out=q_sb[:, :, bank * BANK_TILES : (bank + 1) * BANK_TILES, :],
+                    in0=acc[:].rearrange("p i (h d) -> p h i d", h=HEADS),
+                    in1=bias_bank[:],
+                    op=ALU.add,
+                )
+
+            sumsq = small.tile([P, HEADS, TILES], F32)
+            for h in range(HEADS):
+                for j in range(TILES):
+                    nc.scalar.activation(
+                        out=squares[:],
+                        in_=q_sb[:, h, j, :],
+                        func=ACT.Square,
+                        accum_out=sumsq[:, h, j : j + 1],
+                    )
+            norm = small.tile([P, HEADS, TILES], F32)
+            nc.scalar.activation(out=norm[:], in_=sumsq[:], func=ACT.Sqrt)
+            gain = small.tile([P, HEADS, TILES], F32)
+            nc.vector.reciprocal(out=gain[:], in_=norm[:])
+            nc.vector.tensor_tensor(out=gain[:], in0=gain[:], in1=gamma_chunk[:], op=ALU.mult)
+
+            nc.gpsimd.tensor_tensor(
+                out=q_sb[:],
+                in0=q_sb[:],
+                in1=gain[:].unsqueeze(3).to_broadcast([P, HEADS, TILES, HEAD_DIM]),
+                op=ALU.mult,
+            )
+
+            b = c // CHUNKS_PER_BATCH
+            n0 = (c % CHUNKS_PER_BATCH) * CHUNK_TOKENS
+            nc.sync.dma_start(
+                out=out[b, :, n0 : n0 + CHUNK_TOKENS, :].rearrange(
+                    "h (p j) d -> p h (j d)", j=TILES
+                ),
+                in_=q_sb[:].rearrange("p h j d -> p h (j d)"),
+            )

@@ -18,13 +18,16 @@ OUT_COLS = HEADS * HEAD_DIM
 PACK = 4
 WORDS = K // 2
 
-TILES = 8
-CHUNK_TOKENS = P * TILES
-CHUNKS = BATCH * TOKENS // CHUNK_TOKENS
+CHUNK_TILES = 8
+CHUNK_TOKENS = P * CHUNK_TILES
 CHUNKS_PER_BATCH = TOKENS // CHUNK_TOKENS
+ROUND_TILES = 4
+ROUNDS_PER_CHUNK = CHUNK_TILES // ROUND_TILES
+ROUNDS = BATCH * TOKENS // (P * ROUND_TILES)
 BANK_TILES = 2
-BANKS = TILES // BANK_TILES
-QUANT_TILES = 4
+BANKS = ROUND_TILES // BANK_TILES
+LOAD_AHEAD = 6
+GPSIMD_TILES = 2
 
 FLOPS = 2 * BATCH * TOKENS * K * OUT_COLS
 
@@ -32,21 +35,29 @@ FLOPS = 2 * BATCH * TOKENS * K * OUT_COLS
 def tile_ufoattention_pb_t_kernel(tc, queries, Wq, bq, gamma, out):
     nc = tc.nc
     with ExitStack() as ctx:
+        ctx.enter_context(tc.manual_schedule())
         const = ctx.enter_context(tc.tile_pool(name="const", bufs=1))
-        x_pool = ctx.enter_context(tc.tile_pool(name="x", bufs=6))
+        x_pool = ctx.enter_context(tc.tile_pool(name="x", bufs=LOAD_AHEAD + 2))
         mx_pool = ctx.enter_context(tc.tile_pool(name="mx", bufs=3))
         q_pool = ctx.enter_context(tc.tile_pool(name="q", bufs=4))
-        small = ctx.enter_context(tc.tile_pool(name="small", bufs=3))
-        psum_t = ctx.enter_context(tc.psum_pool(name="psum_t", bufs=4))
-        psum_q = ctx.enter_context(tc.psum_pool(name="psum_q", bufs=4))
+        small = ctx.enter_context(tc.tile_pool(name="small", bufs=6))
+        sq_pool = ctx.enter_context(tc.tile_pool(name="sq", bufs=2))
+        psum_t = ctx.enter_context(tc.psum_pool(name="psum_t", bufs=2 * BANKS))
+        psum_q = ctx.enter_context(tc.psum_pool(name="psum_q", bufs=2 * BANKS))
 
-        x_chunks = queries.flatten_outer_dims().rearrange(
-            "(c p j) k -> c p (j k)", p=P, j=TILES
+        x_rounds = queries.flatten_outer_dims().rearrange(
+            "(c p g i) k -> c g p (i k)", p=P, g=ROUNDS_PER_CHUNK, i=ROUND_TILES
         )
 
-        one = const.tile([P, 1], F32)
-        nc.vector.memset(one[:], 1.0)
-        nc.scalar.activation(out=one[:], in_=one[:], func=ACT.Sqrt)
+        x_tiles, xt_banks, grouped_tiles, code_tiles, scale_tiles = {}, {}, {}, {}, {}
+        acc_banks, q_tiles, sumsq_tiles, norm_tiles = {}, {}, {}, {}
+
+        def load(r):
+            x_tiles[r] = x_pool.tile([P, ROUND_TILES * K], BF16, name="x_sb")
+            nc.sync.dma_start(out=x_tiles[r][:], in_=x_rounds[r // ROUNDS_PER_CHUNK, r % ROUNDS_PER_CHUNK])
+
+        for r in range(LOAD_AHEAD):
+            load(r)
 
         ident = const.tile([P, P], F32)
         make_identity(nc, ident[:])
@@ -56,6 +67,18 @@ def tile_ufoattention_pb_t_kernel(tc, queries, Wq, bq, gamma, out):
             out=w_raw[:].rearrange("p (u e) c -> p u (e c)", u=2),
             in_=Wq.rearrange("(u p e) c -> p u (e c)", u=2, e=2),
         )
+        bias_bf = const.tile([P, OUT_COLS], BF16)
+        nc.scalar.dma_start(out=bias_bf[:], in_=bq.partition_broadcast(P))
+        gamma_bf = const.tile([P, HEADS], BF16)
+        nc.scalar.dma_start(
+            out=gamma_bf[:],
+            in_=gamma.rearrange("a h b c -> (a h b c)").partition_broadcast(P),
+        )
+
+        one = const.tile([P, 1], F32)
+        nc.vector.memset(one[:], 1.0)
+        nc.scalar.activation(out=one[:], in_=one[:], func=ACT.Sqrt)
+
         w_grouped = const.tile([P, OUT_COLS, PACK], BF16, align_bytes=64)
         nc.vector.tensor_copy(out=w_grouped[:], in_=w_raw[:].rearrange("p t c -> p c t"))
         w_codes = const.tile([P, OUT_COLS], U32, align_bytes=64)
@@ -65,43 +88,33 @@ def tile_ufoattention_pb_t_kernel(tc, queries, Wq, bq, gamma, out):
             scales=w_scales[:],
             in_=w_grouped[:].rearrange("p c t -> p (c t)"),
         )
-
-        bias_bf = const.tile([P, OUT_COLS], BF16)
-        nc.scalar.dma_start(out=bias_bf[:], in_=bq.partition_broadcast(P))
         bias_bank = const.tile([P, HEADS, BANK_TILES, HEAD_DIM], F32)
         for i in range(BANK_TILES):
             nc.vector.tensor_copy(
                 out=bias_bank[:, :, i, :],
                 in_=bias_bf[:].rearrange("p (h d) -> p h d", h=HEADS),
             )
-
-        gamma_bf = const.tile([P, HEADS], BF16)
-        nc.scalar.dma_start(
-            out=gamma_bf[:],
-            in_=gamma.rearrange("a h b c -> (a h b c)").partition_broadcast(P),
-        )
-        gamma_chunk = const.tile([P, HEADS, TILES], F32)
+        gamma_round = const.tile([P, HEADS, ROUND_TILES], F32)
         nc.vector.tensor_copy(
-            out=gamma_chunk[:],
-            in_=gamma_bf[:].unsqueeze(2).to_broadcast([P, HEADS, TILES]),
+            out=gamma_round[:],
+            in_=gamma_bf[:].unsqueeze(2).to_broadcast([P, HEADS, ROUND_TILES]),
         )
 
-        squares = const.tile([P, HEAD_DIM], F32)
-
-        for c in range(CHUNKS):
-            x_sb = x_pool.tile([P, TILES * K], BF16)
-            nc.sync.dma_start(out=x_sb[:], in_=x_chunks[c])
-            x_words = x_sb[:].bitcast(F32)
-
-            grouped = mx_pool.tile([P, TILES * K], BF16, align_bytes=64)
-            grouped_words = grouped[:].bitcast(F32)
+        def transpose(r):
+            x_words = x_tiles[r][:].bitcast(F32)
+            xt_banks[r] = []
             for bank in range(BANKS):
-                xt = psum_t.tile([P, BANK_TILES, 2, P], F32)
+                xt = psum_t.tile([P, BANK_TILES, 2, P], F32, name="xt")
                 for i in range(BANK_TILES):
-                    j = bank * BANK_TILES + i
                     for u in range(2):
-                        first = j * WORDS + u * P
+                        first = (bank * BANK_TILES + i) * WORDS + u * P
                         nc.tensor.transpose(xt[:, i, u, :], x_words[:, first : first + P], ident[:])
+                xt_banks[r].append(xt)
+
+        def regroup(r):
+            grouped_tiles[r] = mx_pool.tile([P, ROUND_TILES * K], BF16, align_bytes=64, name="grouped")
+            grouped_words = grouped_tiles[r][:].bitcast(F32)
+            for bank, xt in enumerate(xt_banks[r]):
                 dst = grouped_words[
                     :, bank * BANK_TILES * WORDS : (bank + 1) * BANK_TILES * WORDS
                 ].rearrange("p (i r u) -> p i r u", i=BANK_TILES, u=2)
@@ -111,64 +124,112 @@ def tile_ufoattention_pb_t_kernel(tc, queries, Wq, bq, gamma, out):
                 else:
                     nc.vector.tensor_copy(out=dst, in_=src)
 
-            codes = mx_pool.tile([P, TILES * P], U32, align_bytes=64)
-            scales = mx_pool.tile([P, TILES * P], U8, align_bytes=64)
-            for g in range(TILES // QUANT_TILES):
-                cols = slice(g * QUANT_TILES * P, (g + 1) * QUANT_TILES * P)
-                nc.vector.quantize_mx(
-                    out=codes[:, cols].bitcast(FP8X4),
-                    scales=scales[:, cols],
-                    in_=grouped[:, g * QUANT_TILES * K : (g + 1) * QUANT_TILES * K],
-                )
+        def quantise(r):
+            code_tiles[r] = mx_pool.tile([P, ROUND_TILES * P], U32, align_bytes=64, name="codes")
+            scale_tiles[r] = mx_pool.tile([P, ROUND_TILES * P], U8, align_bytes=64, name="scales")
+            nc.vector.quantize_mx(
+                out=code_tiles[r][:].bitcast(FP8X4),
+                scales=scale_tiles[r][:],
+                in_=grouped_tiles[r][:],
+            )
 
-            q_sb = q_pool.tile([P, HEADS, TILES, HEAD_DIM], F32)
+        def project(r):
+            codes, scales = code_tiles[r], scale_tiles[r]
+            acc_banks[r] = []
             for bank in range(BANKS):
-                acc = psum_q.tile([P, BANK_TILES, OUT_COLS], F32)
+                acc = psum_q.tile([P, BANK_TILES, OUT_COLS], F32, name="acc")
                 for i in range(BANK_TILES):
-                    j = bank * BANK_TILES + i
+                    cols = slice((bank * BANK_TILES + i) * P, (bank * BANK_TILES + i + 1) * P)
                     nc.tensor.matmul_mx(
                         out=acc[:, i, :],
-                        lhsT=codes[:, j * P : (j + 1) * P].bitcast(FP8X4),
-                        lhsT_scale=scales[:, j * P : (j + 1) * P],
+                        lhsT=codes[:, cols].bitcast(FP8X4),
+                        lhsT_scale=scales[:, cols],
                         rhs=w_codes[:].bitcast(FP8X4),
                         rhs_scale=w_scales[:],
                         start=True,
                         stop=True,
                     )
+                acc_banks[r].append(acc)
+
+        def q_of_round(r):
+            first = (r % ROUNDS_PER_CHUNK) * ROUND_TILES
+            return q_tiles[r // ROUNDS_PER_CHUNK][:, :, first : first + ROUND_TILES, :]
+
+        def add_bias(r):
+            if r % ROUNDS_PER_CHUNK == 0:
+                q_tiles[r // ROUNDS_PER_CHUNK] = q_pool.tile(
+                    [P, HEADS, CHUNK_TILES, HEAD_DIM], F32, name="q_sb"
+                )
+            q_round = q_of_round(r)
+            for bank, acc in enumerate(acc_banks[r]):
                 nc.vector.tensor_tensor(
-                    out=q_sb[:, :, bank * BANK_TILES : (bank + 1) * BANK_TILES, :],
+                    out=q_round[:, :, bank * BANK_TILES : (bank + 1) * BANK_TILES, :],
                     in0=acc[:].rearrange("p i (h d) -> p h i d", h=HEADS),
                     in1=bias_bank[:],
                     op=ALU.add,
                 )
 
-            sumsq = small.tile([P, HEADS, TILES], F32)
+        def norms(r):
+            q_round = q_of_round(r)
+            sumsq = small.tile([P, HEADS, ROUND_TILES], F32, name="sumsq")
+            squares = sq_pool.tile([P, HEADS, ROUND_TILES, HEAD_DIM], F32, name="squares")
             for h in range(HEADS):
-                for j in range(TILES):
+                for i in range(ROUND_TILES):
                     nc.scalar.activation(
-                        out=squares[:],
-                        in_=q_sb[:, h, j, :],
+                        out=squares[:, h, i, :],
+                        in_=q_round[:, h, i, :],
                         func=ACT.Square,
-                        accum_out=sumsq[:, h, j : j + 1],
+                        accum_out=sumsq[:, h, i : i + 1],
                     )
-            norm = small.tile([P, HEADS, TILES], F32)
-            nc.scalar.activation(out=norm[:], in_=sumsq[:], func=ACT.Sqrt)
-            gain = small.tile([P, HEADS, TILES], F32)
-            nc.vector.reciprocal(out=gain[:], in_=norm[:])
-            nc.vector.tensor_tensor(out=gain[:], in0=gain[:], in1=gamma_chunk[:], op=ALU.mult)
+            norm_tiles[r] = small.tile([P, HEADS, ROUND_TILES], F32, name="norm")
+            nc.scalar.activation(out=norm_tiles[r][:], in_=sumsq[:], func=ACT.Sqrt)
 
+        def scale(r):
+            q_round = q_of_round(r)
+            gain = small.tile([P, HEADS, ROUND_TILES], F32, name="gain")
+            nc.vector.reciprocal(out=gain[:], in_=norm_tiles[r][:])
+            nc.vector.tensor_tensor(out=gain[:], in0=gain[:], in1=gamma_round[:], op=ALU.mult)
             nc.gpsimd.tensor_tensor(
-                out=q_sb[:],
-                in0=q_sb[:],
-                in1=gain[:].unsqueeze(3).to_broadcast([P, HEADS, TILES, HEAD_DIM]),
+                out=q_round[:, :, 0:GPSIMD_TILES, :],
+                in0=q_round[:, :, 0:GPSIMD_TILES, :],
+                in1=gain[:, :, 0:GPSIMD_TILES].unsqueeze(3).to_broadcast(
+                    [P, HEADS, GPSIMD_TILES, HEAD_DIM]
+                ),
                 op=ALU.mult,
             )
+            for i in range(GPSIMD_TILES, ROUND_TILES):
+                for h in range(HEADS):
+                    nc.vector.tensor_scalar_mul(
+                        out=q_round[:, h, i, :], in0=q_round[:, h, i, :], scalar1=gain[:, h, i : i + 1]
+                    )
 
+        def store(c):
             b = c // CHUNKS_PER_BATCH
             n0 = (c % CHUNKS_PER_BATCH) * CHUNK_TOKENS
             nc.sync.dma_start(
                 out=out[b, :, n0 : n0 + CHUNK_TOKENS, :].rearrange(
-                    "h (p j) d -> p h (j d)", j=TILES
+                    "h (p j) d -> p h (j d)", j=CHUNK_TILES
                 ),
-                in_=q_sb[:].rearrange("p h j d -> p h (j d)"),
+                in_=q_tiles[c][:].rearrange("p h j d -> p h (j d)"),
             )
+
+        transpose(0)
+        for s in range(ROUNDS + 4):
+            if s + LOAD_AHEAD < ROUNDS:
+                load(s + LOAD_AHEAD)
+            if 0 <= s - 2 < ROUNDS:
+                project(s - 2)
+            if s + 1 < ROUNDS:
+                transpose(s + 1)
+            if 0 <= s - 1 < ROUNDS:
+                quantise(s - 1)
+            if 0 <= s - 4 < ROUNDS:
+                scale(s - 4)
+            if s < ROUNDS:
+                regroup(s)
+            if 0 <= s - 2 < ROUNDS:
+                add_bias(s - 2)
+            if 0 <= s - 3 < ROUNDS:
+                norms(s - 3)
+            if 0 <= s - 4 < ROUNDS and (s - 4) % ROUNDS_PER_CHUNK == ROUNDS_PER_CHUNK - 1:
+                store((s - 4) // ROUNDS_PER_CHUNK)

@@ -27,7 +27,6 @@ ROUNDS = BATCH * TOKENS // (P * ROUND_TILES)
 BANK_TILES = 2
 BANKS = ROUND_TILES // BANK_TILES
 LOAD_AHEAD = 6
-GPSIMD_TILES = 2
 
 FLOPS = 2 * BATCH * TOKENS * K * OUT_COLS
 
@@ -39,9 +38,9 @@ def tile_ufoattention_pb_t_kernel(tc, queries, Wq, bq, gamma, out):
         const = ctx.enter_context(tc.tile_pool(name="const", bufs=1))
         x_pool = ctx.enter_context(tc.tile_pool(name="x", bufs=LOAD_AHEAD + 2))
         mx_pool = ctx.enter_context(tc.tile_pool(name="mx", bufs=3))
-        q_pool = ctx.enter_context(tc.tile_pool(name="q", bufs=4))
-        small = ctx.enter_context(tc.tile_pool(name="small", bufs=6))
-        sq_pool = ctx.enter_context(tc.tile_pool(name="sq", bufs=2))
+        q_pool = ctx.enter_context(tc.tile_pool(name="q", bufs=5))
+        small = ctx.enter_context(tc.tile_pool(name="small", bufs=8))
+        sq_pool = ctx.enter_context(tc.tile_pool(name="sq", bufs=3))
         psum_t = ctx.enter_context(tc.psum_pool(name="psum_t", bufs=2 * BANKS))
         psum_q = ctx.enter_context(tc.psum_pool(name="psum_q", bufs=2 * BANKS))
 
@@ -50,7 +49,7 @@ def tile_ufoattention_pb_t_kernel(tc, queries, Wq, bq, gamma, out):
         )
 
         x_tiles, xt_banks, grouped_tiles, code_tiles, scale_tiles = {}, {}, {}, {}, {}
-        acc_banks, q_tiles, sumsq_tiles, norm_tiles = {}, {}, {}, {}
+        acc_banks, q_tiles, square_tiles, sumsq_tiles, rnorm_tiles = {}, {}, {}, {}, {}
 
         def load(r):
             x_tiles[r] = x_pool.tile([P, ROUND_TILES * K], BF16, name="x_sb")
@@ -77,7 +76,7 @@ def tile_ufoattention_pb_t_kernel(tc, queries, Wq, bq, gamma, out):
 
         one = const.tile([P, 1], F32)
         nc.vector.memset(one[:], 1.0)
-        nc.scalar.activation(out=one[:], in_=one[:], func=ACT.Sqrt)
+        nc.scalar.activation(out=one[:], in_=one[:], func=ACT.Abs_reciprocal_sqrt)
 
         w_grouped = const.tile([P, OUT_COLS, PACK], BF16, align_bytes=64)
         nc.vector.tensor_copy(out=w_grouped[:], in_=w_raw[:].rearrange("p t c -> p c t"))
@@ -119,10 +118,7 @@ def tile_ufoattention_pb_t_kernel(tc, queries, Wq, bq, gamma, out):
                     :, bank * BANK_TILES * WORDS : (bank + 1) * BANK_TILES * WORDS
                 ].rearrange("p (i r u) -> p i r u", i=BANK_TILES, u=2)
                 src = xt[:].rearrange("p i u r -> p i r u")
-                if bank % 2 == 0:
-                    nc.scalar.copy(out=dst, in_=src)
-                else:
-                    nc.vector.tensor_copy(out=dst, in_=src)
+                nc.scalar.copy(out=dst, in_=src)
 
         def quantise(r):
             code_tiles[r] = mx_pool.tile([P, ROUND_TILES * P], U32, align_bytes=64, name="codes")
@@ -169,39 +165,32 @@ def tile_ufoattention_pb_t_kernel(tc, queries, Wq, bq, gamma, out):
                     op=ALU.add,
                 )
 
-        def norms(r):
-            q_round = q_of_round(r)
-            sumsq = small.tile([P, HEADS, ROUND_TILES], F32, name="sumsq")
-            squares = sq_pool.tile([P, HEADS, ROUND_TILES, HEAD_DIM], F32, name="squares")
-            for h in range(HEADS):
-                for i in range(ROUND_TILES):
-                    nc.scalar.activation(
-                        out=squares[:, h, i, :],
-                        in_=q_round[:, h, i, :],
-                        func=ACT.Square,
-                        accum_out=sumsq[:, h, i : i + 1],
-                    )
-            norm_tiles[r] = small.tile([P, HEADS, ROUND_TILES], F32, name="norm")
-            nc.scalar.activation(out=norm_tiles[r][:], in_=sumsq[:], func=ACT.Sqrt)
+        def square(r):
+            square_tiles[r] = sq_pool.tile([P, HEADS, ROUND_TILES, HEAD_DIM], F32, name="squares")
+            nc.scalar.activation(out=square_tiles[r][:], in_=q_of_round(r), func=ACT.Square)
+
+        def sum_squares(r):
+            sumsq_tiles[r] = small.tile([P, HEADS, ROUND_TILES], F32, name="sumsq")
+            nc.vector.tensor_reduce(
+                out=sumsq_tiles[r][:], in_=square_tiles[r][:], axis=mybir.AxisListType.X, op=ALU.add
+            )
+
+        def reciprocal_norm(r):
+            rnorm_tiles[r] = small.tile([P, HEADS, ROUND_TILES], F32, name="rnorm")
+            nc.scalar.activation(
+                out=rnorm_tiles[r][:], in_=sumsq_tiles[r][:], func=ACT.Abs_reciprocal_sqrt
+            )
 
         def scale(r):
             q_round = q_of_round(r)
             gain = small.tile([P, HEADS, ROUND_TILES], F32, name="gain")
-            nc.vector.reciprocal(out=gain[:], in_=norm_tiles[r][:])
-            nc.vector.tensor_tensor(out=gain[:], in0=gain[:], in1=gamma_round[:], op=ALU.mult)
+            nc.vector.tensor_tensor(out=gain[:], in0=rnorm_tiles[r][:], in1=gamma_round[:], op=ALU.mult)
             nc.gpsimd.tensor_tensor(
-                out=q_round[:, :, 0:GPSIMD_TILES, :],
-                in0=q_round[:, :, 0:GPSIMD_TILES, :],
-                in1=gain[:, :, 0:GPSIMD_TILES].unsqueeze(3).to_broadcast(
-                    [P, HEADS, GPSIMD_TILES, HEAD_DIM]
-                ),
+                out=q_round,
+                in0=q_round,
+                in1=gain[:].unsqueeze(3).to_broadcast([P, HEADS, ROUND_TILES, HEAD_DIM]),
                 op=ALU.mult,
             )
-            for i in range(GPSIMD_TILES, ROUND_TILES):
-                for h in range(HEADS):
-                    nc.vector.tensor_scalar_mul(
-                        out=q_round[:, h, i, :], in0=q_round[:, h, i, :], scalar1=gain[:, h, i : i + 1]
-                    )
 
         def store(c):
             b = c // CHUNKS_PER_BATCH
@@ -214,7 +203,7 @@ def tile_ufoattention_pb_t_kernel(tc, queries, Wq, bq, gamma, out):
             )
 
         transpose(0)
-        for s in range(ROUNDS + 4):
+        for s in range(ROUNDS + 6):
             if s + LOAD_AHEAD < ROUNDS:
                 load(s + LOAD_AHEAD)
             if 0 <= s - 2 < ROUNDS:
@@ -223,13 +212,17 @@ def tile_ufoattention_pb_t_kernel(tc, queries, Wq, bq, gamma, out):
                 transpose(s + 1)
             if 0 <= s - 1 < ROUNDS:
                 quantise(s - 1)
-            if 0 <= s - 4 < ROUNDS:
-                scale(s - 4)
+            if 0 <= s - 6 < ROUNDS:
+                scale(s - 6)
             if s < ROUNDS:
                 regroup(s)
             if 0 <= s - 2 < ROUNDS:
                 add_bias(s - 2)
             if 0 <= s - 3 < ROUNDS:
-                norms(s - 3)
-            if 0 <= s - 4 < ROUNDS and (s - 4) % ROUNDS_PER_CHUNK == ROUNDS_PER_CHUNK - 1:
-                store((s - 4) // ROUNDS_PER_CHUNK)
+                square(s - 3)
+            if 0 <= s - 4 < ROUNDS:
+                sum_squares(s - 4)
+            if 0 <= s - 5 < ROUNDS:
+                reciprocal_norm(s - 5)
+            if 0 <= s - 6 < ROUNDS and (s - 6) % ROUNDS_PER_CHUNK == ROUNDS_PER_CHUNK - 1:
+                store((s - 6) // ROUNDS_PER_CHUNK)

@@ -27,6 +27,7 @@ ROUNDS = BATCH * TOKENS // (P * ROUND_TILES)
 BANK_TILES = 2
 BANKS = ROUND_TILES // BANK_TILES
 LOAD_AHEAD = 6
+GPSIMD_TILES = 3
 
 FLOPS = 2 * BATCH * TOKENS * K * OUT_COLS
 
@@ -38,8 +39,8 @@ def tile_ufoattention_pb_t_kernel(tc, queries, Wq, bq, gamma, out):
         const = ctx.enter_context(tc.tile_pool(name="const", bufs=1))
         x_pool = ctx.enter_context(tc.tile_pool(name="x", bufs=LOAD_AHEAD + 2))
         mx_pool = ctx.enter_context(tc.tile_pool(name="mx", bufs=3))
-        q_pool = ctx.enter_context(tc.tile_pool(name="q", bufs=5))
-        small = ctx.enter_context(tc.tile_pool(name="small", bufs=8))
+        q_pool = ctx.enter_context(tc.tile_pool(name="q", bufs=6))
+        small = ctx.enter_context(tc.tile_pool(name="small", bufs=10))
         sq_pool = ctx.enter_context(tc.tile_pool(name="sq", bufs=3))
         psum_t = ctx.enter_context(tc.psum_pool(name="psum_t", bufs=2 * BANKS))
         psum_q = ctx.enter_context(tc.psum_pool(name="psum_q", bufs=2 * BANKS))
@@ -49,7 +50,7 @@ def tile_ufoattention_pb_t_kernel(tc, queries, Wq, bq, gamma, out):
         )
 
         x_tiles, xt_banks, grouped_tiles, code_tiles, scale_tiles = {}, {}, {}, {}, {}
-        acc_banks, q_tiles, square_tiles, sumsq_tiles, rnorm_tiles = {}, {}, {}, {}, {}
+        acc_banks, q_tiles, square_tiles, sumsq_tiles, rnorm_tiles, gain_tiles = {}, {}, {}, {}, {}, {}
 
         def load(r):
             x_tiles[r] = x_pool.tile([P, ROUND_TILES * K], BF16, name="x_sb")
@@ -181,16 +182,30 @@ def tile_ufoattention_pb_t_kernel(tc, queries, Wq, bq, gamma, out):
                 out=rnorm_tiles[r][:], in_=sumsq_tiles[r][:], func=ACT.Abs_reciprocal_sqrt
             )
 
+        def gains(r):
+            gain_tiles[r] = small.tile([P, HEADS, ROUND_TILES], F32, name="gain")
+            nc.vector.tensor_tensor(
+                out=gain_tiles[r][:], in0=rnorm_tiles[r][:], in1=gamma_round[:], op=ALU.mult
+            )
+
         def scale(r):
-            q_round = q_of_round(r)
-            gain = small.tile([P, HEADS, ROUND_TILES], F32, name="gain")
-            nc.vector.tensor_tensor(out=gain[:], in0=rnorm_tiles[r][:], in1=gamma_round[:], op=ALU.mult)
+            q_round, gain = q_of_round(r), gain_tiles[r]
             nc.gpsimd.tensor_tensor(
-                out=q_round,
-                in0=q_round,
-                in1=gain[:].unsqueeze(3).to_broadcast([P, HEADS, ROUND_TILES, HEAD_DIM]),
+                out=q_round[:, :, 0:GPSIMD_TILES, :],
+                in0=q_round[:, :, 0:GPSIMD_TILES, :],
+                in1=gain[:, :, 0:GPSIMD_TILES].unsqueeze(3).to_broadcast(
+                    [P, HEADS, GPSIMD_TILES, HEAD_DIM]
+                ),
                 op=ALU.mult,
             )
+            for i in range(GPSIMD_TILES, ROUND_TILES):
+                for h in range(HEADS):
+                    nc.scalar.activation(
+                        out=q_round[:, h, i, :],
+                        in_=q_round[:, h, i, :],
+                        func=ACT.Copy,
+                        scale=gain[:, h, i : i + 1],
+                    )
 
         def store(c):
             b = c // CHUNKS_PER_BATCH
@@ -203,26 +218,28 @@ def tile_ufoattention_pb_t_kernel(tc, queries, Wq, bq, gamma, out):
             )
 
         transpose(0)
-        for s in range(ROUNDS + 6):
+        for s in range(ROUNDS + 7):
             if s + LOAD_AHEAD < ROUNDS:
                 load(s + LOAD_AHEAD)
             if 0 <= s - 2 < ROUNDS:
                 project(s - 2)
             if s + 1 < ROUNDS:
                 transpose(s + 1)
-            if 0 <= s - 1 < ROUNDS:
-                quantise(s - 1)
-            if 0 <= s - 6 < ROUNDS:
-                scale(s - 6)
+            if 0 <= s - 7 < ROUNDS:
+                gains(s - 7)
             if s < ROUNDS:
                 regroup(s)
-            if 0 <= s - 2 < ROUNDS:
-                add_bias(s - 2)
             if 0 <= s - 3 < ROUNDS:
-                square(s - 3)
+                add_bias(s - 3)
             if 0 <= s - 4 < ROUNDS:
-                sum_squares(s - 4)
+                square(s - 4)
             if 0 <= s - 5 < ROUNDS:
-                reciprocal_norm(s - 5)
-            if 0 <= s - 6 < ROUNDS and (s - 6) % ROUNDS_PER_CHUNK == ROUNDS_PER_CHUNK - 1:
-                store((s - 6) // ROUNDS_PER_CHUNK)
+                sum_squares(s - 5)
+            if 0 <= s - 6 < ROUNDS:
+                reciprocal_norm(s - 6)
+            if 0 <= s - 7 < ROUNDS:
+                scale(s - 7)
+            if 0 <= s - 1 < ROUNDS:
+                quantise(s - 1)
+            if 0 <= s - 7 < ROUNDS and (s - 7) % ROUNDS_PER_CHUNK == ROUNDS_PER_CHUNK - 1:
+                store((s - 7) // ROUNDS_PER_CHUNK)

@@ -18,12 +18,10 @@ OUT_COLS = HEADS * HEAD_DIM
 PACK = 4
 WORDS = K // 2
 
-CHUNK_TILES = 8
-CHUNK_TOKENS = P * CHUNK_TILES
-CHUNKS_PER_BATCH = TOKENS // CHUNK_TOKENS
 ROUND_TILES = 4
-ROUNDS_PER_CHUNK = CHUNK_TILES // ROUND_TILES
-ROUNDS = BATCH * TOKENS // (P * ROUND_TILES)
+ROUND_TOKENS = P * ROUND_TILES
+ROUNDS_PER_BATCH = TOKENS // ROUND_TOKENS
+ROUNDS = BATCH * ROUNDS_PER_BATCH
 BANK_TILES = 2
 BANKS = ROUND_TILES // BANK_TILES
 LOAD_AHEAD = 6
@@ -39,14 +37,14 @@ def tile_ufoattention_pb_t_kernel(tc, queries, Wq, bq, gamma, out):
         const = ctx.enter_context(tc.tile_pool(name="const", bufs=1))
         x_pool = ctx.enter_context(tc.tile_pool(name="x", bufs=LOAD_AHEAD + 2))
         mx_pool = ctx.enter_context(tc.tile_pool(name="mx", bufs=3))
-        q_pool = ctx.enter_context(tc.tile_pool(name="q", bufs=6))
+        q_pool = ctx.enter_context(tc.tile_pool(name="q", bufs=8))
         small = ctx.enter_context(tc.tile_pool(name="small", bufs=10))
         sq_pool = ctx.enter_context(tc.tile_pool(name="sq", bufs=3))
         psum_t = ctx.enter_context(tc.psum_pool(name="psum_t", bufs=2 * BANKS))
         psum_q = ctx.enter_context(tc.psum_pool(name="psum_q", bufs=2 * BANKS))
 
         x_rounds = queries.flatten_outer_dims().rearrange(
-            "(c p g i) k -> c g p (i k)", p=P, g=ROUNDS_PER_CHUNK, i=ROUND_TILES
+            "(r p i) k -> r p (i k)", p=P, i=ROUND_TILES
         )
 
         x_tiles, xt_banks, grouped_tiles, code_tiles, scale_tiles = {}, {}, {}, {}, {}
@@ -54,7 +52,7 @@ def tile_ufoattention_pb_t_kernel(tc, queries, Wq, bq, gamma, out):
 
         def load(r):
             x_tiles[r] = x_pool.tile([P, ROUND_TILES * K], BF16, name="x_sb")
-            nc.sync.dma_start(out=x_tiles[r][:], in_=x_rounds[r // ROUNDS_PER_CHUNK, r % ROUNDS_PER_CHUNK])
+            nc.sync.dma_start(out=x_tiles[r][:], in_=x_rounds[r])
 
         for r in range(LOAD_AHEAD):
             load(r)
@@ -148,16 +146,9 @@ def tile_ufoattention_pb_t_kernel(tc, queries, Wq, bq, gamma, out):
                     )
                 acc_banks[r].append(acc)
 
-        def q_of_round(r):
-            first = (r % ROUNDS_PER_CHUNK) * ROUND_TILES
-            return q_tiles[r // ROUNDS_PER_CHUNK][:, :, first : first + ROUND_TILES, :]
-
         def add_bias(r):
-            if r % ROUNDS_PER_CHUNK == 0:
-                q_tiles[r // ROUNDS_PER_CHUNK] = q_pool.tile(
-                    [P, HEADS, CHUNK_TILES, HEAD_DIM], F32, name="q_sb"
-                )
-            q_round = q_of_round(r)
+            q_tiles[r] = q_pool.tile([P, HEADS, ROUND_TILES, HEAD_DIM], F32, name="q_sb")
+            q_round = q_tiles[r]
             for bank, acc in enumerate(acc_banks[r]):
                 nc.vector.tensor_tensor(
                     out=q_round[:, :, bank * BANK_TILES : (bank + 1) * BANK_TILES, :],
@@ -168,7 +159,7 @@ def tile_ufoattention_pb_t_kernel(tc, queries, Wq, bq, gamma, out):
 
         def square(r):
             square_tiles[r] = sq_pool.tile([P, HEADS, ROUND_TILES, HEAD_DIM], F32, name="squares")
-            nc.scalar.activation(out=square_tiles[r][:], in_=q_of_round(r), func=ACT.Square)
+            nc.scalar.activation(out=square_tiles[r][:], in_=q_tiles[r][:], func=ACT.Square)
 
         def sum_squares(r):
             sumsq_tiles[r] = small.tile([P, HEADS, ROUND_TILES], F32, name="sumsq")
@@ -189,7 +180,7 @@ def tile_ufoattention_pb_t_kernel(tc, queries, Wq, bq, gamma, out):
             )
 
         def scale(r):
-            q_round, gain = q_of_round(r), gain_tiles[r]
+            q_round, gain = q_tiles[r], gain_tiles[r]
             nc.gpsimd.tensor_tensor(
                 out=q_round[:, :, 0:GPSIMD_TILES, :],
                 in0=q_round[:, :, 0:GPSIMD_TILES, :],
@@ -207,26 +198,28 @@ def tile_ufoattention_pb_t_kernel(tc, queries, Wq, bq, gamma, out):
                         scale=gain[:, h, i : i + 1],
                     )
 
-        def store(c):
-            b = c // CHUNKS_PER_BATCH
-            n0 = (c % CHUNKS_PER_BATCH) * CHUNK_TOKENS
+        def store(r):
+            b = r // ROUNDS_PER_BATCH
+            n0 = (r % ROUNDS_PER_BATCH) * ROUND_TOKENS
             nc.sync.dma_start(
-                out=out[b, :, n0 : n0 + CHUNK_TOKENS, :].rearrange(
-                    "h (p j) d -> p h (j d)", j=CHUNK_TILES
+                out=out[b, :, n0 : n0 + ROUND_TOKENS, :].rearrange(
+                    "h (p i) d -> p h (i d)", i=ROUND_TILES
                 ),
-                in_=q_tiles[c][:].rearrange("p h j d -> p h (j d)"),
+                in_=q_tiles[r][:].rearrange("p h i d -> p h (i d)"),
             )
 
         transpose(0)
-        for s in range(ROUNDS + 7):
+        for s in range(ROUNDS + 6):
             if s + LOAD_AHEAD < ROUNDS:
                 load(s + LOAD_AHEAD)
             if 0 <= s - 2 < ROUNDS:
                 project(s - 2)
             if s + 1 < ROUNDS:
                 transpose(s + 1)
-            if 0 <= s - 7 < ROUNDS:
-                gains(s - 7)
+            if 0 <= s - 6 < ROUNDS:
+                gains(s - 6)
+            if 0 <= s - 5 < ROUNDS:
+                sum_squares(s - 5)
             if s < ROUNDS:
                 regroup(s)
             if 0 <= s - 3 < ROUNDS:
@@ -234,12 +227,10 @@ def tile_ufoattention_pb_t_kernel(tc, queries, Wq, bq, gamma, out):
             if 0 <= s - 4 < ROUNDS:
                 square(s - 4)
             if 0 <= s - 5 < ROUNDS:
-                sum_squares(s - 5)
+                reciprocal_norm(s - 5)
             if 0 <= s - 6 < ROUNDS:
-                reciprocal_norm(s - 6)
-            if 0 <= s - 7 < ROUNDS:
-                scale(s - 7)
+                scale(s - 6)
             if 0 <= s - 1 < ROUNDS:
                 quantise(s - 1)
-            if 0 <= s - 7 < ROUNDS and (s - 7) % ROUNDS_PER_CHUNK == ROUNDS_PER_CHUNK - 1:
-                store((s - 7) // ROUNDS_PER_CHUNK)
+            if 0 <= s - 6 < ROUNDS:
+                store(s - 6)

@@ -25,7 +25,7 @@ ROUNDS = BATCH * ROUNDS_PER_BATCH
 BANK_TILES = 2
 BANKS = ROUND_TILES // BANK_TILES
 LOAD_AHEAD = 6
-GPSIMD_TILES = 3
+GPSIMD_TILES = 4
 
 FLOPS = 2 * BATCH * TOKENS * K * OUT_COLS
 

from contextlib import ExitStack

import concourse.mybir as mybir
from concourse.masks import make_identity

F32 = mybir.dt.float32
BF16 = mybir.dt.bfloat16
U32 = mybir.dt.uint32
U8 = mybir.dt.uint8
FP8X4 = mybir.dt.float8_e4m3fn_x4
ACT = mybir.ActivationFunctionType
ALU = mybir.AluOpType

P = 128
BATCH, TOKENS, K = 4, 4096, 512
HEADS, HEAD_DIM = 4, 64
OUT_COLS = HEADS * HEAD_DIM
PACK = 4
WORDS = K // 2

ROUND_TILES = 4
ROUND_TOKENS = P * ROUND_TILES
ROUNDS_PER_BATCH = TOKENS // ROUND_TOKENS
ROUNDS = BATCH * ROUNDS_PER_BATCH
BANK_TILES = 2
BANKS = ROUND_TILES // BANK_TILES
LOAD_AHEAD = 6
GPSIMD_TILES = 4

FLOPS = 2 * BATCH * TOKENS * K * OUT_COLS


def tile_ufoattention_pb_t_kernel(tc, queries, Wq, bq, gamma, out):
    nc = tc.nc
    with ExitStack() as ctx:
        ctx.enter_context(tc.manual_schedule())
        const = ctx.enter_context(tc.tile_pool(name="const", bufs=1))
        x_pool = ctx.enter_context(tc.tile_pool(name="x", bufs=LOAD_AHEAD + 2))
        mx_pool = ctx.enter_context(tc.tile_pool(name="mx", bufs=3))
        q_pool = ctx.enter_context(tc.tile_pool(name="q", bufs=8))
        small = ctx.enter_context(tc.tile_pool(name="small", bufs=10))
        sq_pool = ctx.enter_context(tc.tile_pool(name="sq", bufs=3))
        psum_t = ctx.enter_context(tc.psum_pool(name="psum_t", bufs=2 * BANKS))
        psum_q = ctx.enter_context(tc.psum_pool(name="psum_q", bufs=2 * BANKS))

        x_rounds = queries.flatten_outer_dims().rearrange(
            "(r p i) k -> r p (i k)", p=P, i=ROUND_TILES
        )

        x_tiles, xt_banks, grouped_tiles, code_tiles, scale_tiles = {}, {}, {}, {}, {}
        acc_banks, q_tiles, square_tiles, sumsq_tiles, rnorm_tiles, gain_tiles = {}, {}, {}, {}, {}, {}

        def load(r):
            x_tiles[r] = x_pool.tile([P, ROUND_TILES * K], BF16, name="x_sb")
            nc.sync.dma_start(out=x_tiles[r][:], in_=x_rounds[r])

        for r in range(LOAD_AHEAD):
            load(r)

        ident = const.tile([P, P], F32)
        make_identity(nc, ident[:])

        w_raw = const.tile([P, PACK, OUT_COLS], BF16)
        nc.scalar.dma_start(
            out=w_raw[:].rearrange("p (u e) c -> p u (e c)", u=2),
            in_=Wq.rearrange("(u p e) c -> p u (e c)", u=2, e=2),
        )
        bias_bf = const.tile([P, OUT_COLS], BF16)
        nc.scalar.dma_start(out=bias_bf[:], in_=bq.partition_broadcast(P))
        gamma_bf = const.tile([P, HEADS], BF16)
        nc.scalar.dma_start(
            out=gamma_bf[:],
            in_=gamma.rearrange("a h b c -> (a h b c)").partition_broadcast(P),
        )

        one = const.tile([P, 1], F32)
        nc.vector.memset(one[:], 1.0)
        nc.scalar.activation(out=one[:], in_=one[:], func=ACT.Abs_reciprocal_sqrt)

        w_grouped = const.tile([P, OUT_COLS, PACK], BF16, align_bytes=64)
        nc.vector.tensor_copy(out=w_grouped[:], in_=w_raw[:].rearrange("p t c -> p c t"))
        w_codes = const.tile([P, OUT_COLS], U32, align_bytes=64)
        w_scales = const.tile([P, OUT_COLS], U8, align_bytes=64)
        nc.vector.quantize_mx(
            out=w_codes[:].bitcast(FP8X4),
            scales=w_scales[:],
            in_=w_grouped[:].rearrange("p c t -> p (c t)"),
        )
        bias_bank = const.tile([P, HEADS, BANK_TILES, HEAD_DIM], F32)
        for i in range(BANK_TILES):
            nc.vector.tensor_copy(
                out=bias_bank[:, :, i, :],
                in_=bias_bf[:].rearrange("p (h d) -> p h d", h=HEADS),
            )
        gamma_round = const.tile([P, HEADS, ROUND_TILES], F32)
        nc.vector.tensor_copy(
            out=gamma_round[:],
            in_=gamma_bf[:].unsqueeze(2).to_broadcast([P, HEADS, ROUND_TILES]),
        )

        def transpose(r):
            x_words = x_tiles[r][:].bitcast(F32)
            xt_banks[r] = []
            for bank in range(BANKS):
                xt = psum_t.tile([P, BANK_TILES, 2, P], F32, name="xt")
                for i in range(BANK_TILES):
                    for u in range(2):
                        first = (bank * BANK_TILES + i) * WORDS + u * P
                        nc.tensor.transpose(xt[:, i, u, :], x_words[:, first : first + P], ident[:])
                xt_banks[r].append(xt)

        def regroup(r):
            grouped_tiles[r] = mx_pool.tile([P, ROUND_TILES * K], BF16, align_bytes=64, name="grouped")
            grouped_words = grouped_tiles[r][:].bitcast(F32)
            for bank, xt in enumerate(xt_banks[r]):
                dst = grouped_words[
                    :, bank * BANK_TILES * WORDS : (bank + 1) * BANK_TILES * WORDS
                ].rearrange("p (i r u) -> p i r u", i=BANK_TILES, u=2)
                src = xt[:].rearrange("p i u r -> p i r u")
                nc.scalar.copy(out=dst, in_=src)

        def quantise(r):
            code_tiles[r] = mx_pool.tile([P, ROUND_TILES * P], U32, align_bytes=64, name="codes")
            scale_tiles[r] = mx_pool.tile([P, ROUND_TILES * P], U8, align_bytes=64, name="scales")
            nc.vector.quantize_mx(
                out=code_tiles[r][:].bitcast(FP8X4),
                scales=scale_tiles[r][:],
                in_=grouped_tiles[r][:],
            )

        def project(r):
            codes, scales = code_tiles[r], scale_tiles[r]
            acc_banks[r] = []
            for bank in range(BANKS):
                acc = psum_q.tile([P, BANK_TILES, OUT_COLS], F32, name="acc")
                for i in range(BANK_TILES):
                    cols = slice((bank * BANK_TILES + i) * P, (bank * BANK_TILES + i + 1) * P)
                    nc.tensor.matmul_mx(
                        out=acc[:, i, :],
                        lhsT=codes[:, cols].bitcast(FP8X4),
                        lhsT_scale=scales[:, cols],
                        rhs=w_codes[:].bitcast(FP8X4),
                        rhs_scale=w_scales[:],
                        start=True,
                        stop=True,
                    )
                acc_banks[r].append(acc)

        def add_bias(r):
            q_tiles[r] = q_pool.tile([P, HEADS, ROUND_TILES, HEAD_DIM], F32, name="q_sb")
            q_round = q_tiles[r]
            for bank, acc in enumerate(acc_banks[r]):
                nc.vector.tensor_tensor(
                    out=q_round[:, :, bank * BANK_TILES : (bank + 1) * BANK_TILES, :],
                    in0=acc[:].rearrange("p i (h d) -> p h i d", h=HEADS),
                    in1=bias_bank[:],
                    op=ALU.add,
                )

        def square(r):
            square_tiles[r] = sq_pool.tile([P, HEADS, ROUND_TILES, HEAD_DIM], F32, name="squares")
            nc.scalar.activation(out=square_tiles[r][:], in_=q_tiles[r][:], func=ACT.Square)

        def sum_squares(r):
            sumsq_tiles[r] = small.tile([P, HEADS, ROUND_TILES], F32, name="sumsq")
            nc.vector.tensor_reduce(
                out=sumsq_tiles[r][:], in_=square_tiles[r][:], axis=mybir.AxisListType.X, op=ALU.add
            )

        def reciprocal_norm(r):
            rnorm_tiles[r] = small.tile([P, HEADS, ROUND_TILES], F32, name="rnorm")
            nc.scalar.activation(
                out=rnorm_tiles[r][:], in_=sumsq_tiles[r][:], func=ACT.Abs_reciprocal_sqrt
            )

        def gains(r):
            gain_tiles[r] = small.tile([P, HEADS, ROUND_TILES], F32, name="gain")
            nc.vector.tensor_tensor(
                out=gain_tiles[r][:], in0=rnorm_tiles[r][:], in1=gamma_round[:], op=ALU.mult
            )

        def scale(r):
            q_round, gain = q_tiles[r], gain_tiles[r]
            nc.gpsimd.tensor_tensor(
                out=q_round[:, :, 0:GPSIMD_TILES, :],
                in0=q_round[:, :, 0:GPSIMD_TILES, :],
                in1=gain[:, :, 0:GPSIMD_TILES].unsqueeze(3).to_broadcast(
                    [P, HEADS, GPSIMD_TILES, HEAD_DIM]
                ),
                op=ALU.mult,
            )
            for i in range(GPSIMD_TILES, ROUND_TILES):
                for h in range(HEADS):
                    nc.scalar.activation(
                        out=q_round[:, h, i, :],
                        in_=q_round[:, h, i, :],
                        func=ACT.Copy,
                        scale=gain[:, h, i : i + 1],
                    )

        def store(r):
            b = r // ROUNDS_PER_BATCH
            n0 = (r % ROUNDS_PER_BATCH) * ROUND_TOKENS
            nc.sync.dma_start(
                out=out[b, :, n0 : n0 + ROUND_TOKENS, :].rearrange(
                    "h (p i) d -> p h (i d)", i=ROUND_TILES
                ),
                in_=q_tiles[r][:].rearrange("p h i d -> p h (i d)"),
            )

        transpose(0)
        for s in range(ROUNDS + 6):
            if s + LOAD_AHEAD < ROUNDS:
                load(s + LOAD_AHEAD)
            if 0 <= s - 2 < ROUNDS:
                project(s - 2)
            if s + 1 < ROUNDS:
                transpose(s + 1)
            if 0 <= s - 6 < ROUNDS:
                gains(s - 6)
            if 0 <= s - 5 < ROUNDS:
                sum_squares(s - 5)
            if s < ROUNDS:
                regroup(s)
            if 0 <= s - 3 < ROUNDS:
                add_bias(s - 3)
            if 0 <= s - 4 < ROUNDS:
                square(s - 4)
            if 0 <= s - 5 < ROUNDS:
                reciprocal_norm(s - 5)
            if 0 <= s - 6 < ROUNDS:
                scale(s - 6)
            if 0 <= s - 1 < ROUNDS:
                quantise(s - 1)
            if 0 <= s - 6 < ROUNDS:
                store(s - 6)
